import numpy as np
import ml_dtypes


def mxq(x, axis, fmt="e4m3"):
    dtype, down = {"e4m3": (ml_dtypes.float8_e4m3fn, 7), "e5m2": (ml_dtypes.float8_e5m2, 14)}[fmt]
    v = np.moveaxis(np.asarray(x, np.float32).astype(ml_dtypes.bfloat16).astype(np.float64), axis, -1)
    blocks = v.reshape(v.shape[:-1] + (-1, 32))
    amax = np.abs(blocks).max(-1, keepdims=True)
    byte = np.maximum(np.where(amax > 0, np.frexp(amax)[1] - 1 + 127, 0) - down, 1)
    scale = np.exp2(byte - 127.0)
    codes = (blocks / scale).astype(np.float32).astype(dtype).astype(np.float64)
    return np.moveaxis((codes * scale).reshape(v.shape), -1, axis)


WIDE = False


def mx_kscale(k):
    if not WIDE:
        return np.ones(k)
    levels = np.array([10, -10, 5, -5, 0])
    a = np.random.permutation(np.resize(levels, k // 512 * 4)).reshape(k // 512, 4)
    idx = np.arange(k)
    return np.exp2(a[idx // 512, idx % 128 // 32])


BF16 = ml_dtypes.bfloat16


def bf(x):
    return np.asarray(x, np.float32).astype(BF16)


def f64(x):
    return np.asarray(x).astype(np.float64)


E2M1 = np.array([0.0, 0.5, 1.0, 1.5, 2.0, 3.0, 4.0, 6.0, -0.0, -0.5, -1.0, -1.5, -2.0, -3.0, -4.0, -6.0])


def pack_weight(w, fmt):
    k, n = w.shape
    w = f64(bf(w)).reshape(k // 32, 32, n)
    amax = np.abs(w).max(1)
    if fmt == "e4m3":
        byte = np.frexp(amax)[1] - 1 + 127 - 7
    else:
        mant, ex = np.frexp(amax / 6.0)
        byte = np.where(mant > 0.5, ex, ex - 1) + 127
    byte = np.clip(np.where(amax > 0, byte, 1), 1, 254)
    scaled = (w * np.exp2(127.0 - byte)[:, None, :]).reshape(k, n).astype(np.float32)
    by_word = np.ascontiguousarray(scaled.reshape(k // 512, 128, 4, n).transpose(0, 1, 3, 2))
    if fmt == "e4m3":
        words = by_word.astype(ml_dtypes.float8_e4m3fn).view(np.uint8)
    else:
        c = by_word.astype(ml_dtypes.float4_e2m1fn).view(np.uint8) & 0xF
        words = c[..., 0::2] | (c[..., 1::2] << 4)
    return np.ascontiguousarray(words), np.ascontiguousarray(byte.astype(np.uint8).reshape(k // 512, 16, n))


def unpack_weight(words, scales, fmt):
    g, p, n, _ = words.shape
    if fmt == "e4m3":
        vals = np.ascontiguousarray(words).view(ml_dtypes.float8_e4m3fn).astype(np.float64)
    else:
        nib = np.empty((g, p, n, 4), np.uint8)
        nib[..., 0::2] = words & 0xF
        nib[..., 1::2] = words >> 4
        vals = E2M1[nib]
    vals = vals * np.repeat(np.exp2(scales.astype(np.float64) - 127.0), 8, axis=1)[..., None]
    return vals.transpose(0, 1, 3, 2).reshape(g * 512, n)

def pack4(w):
    words, scales = pack_weight(w, "e2m1")
    return words.reshape(words.shape[0], 128, -1), scales


def unpack4(words, scales):
    return unpack_weight(words.reshape(words.shape[0], 128, -1, 2), scales, "e2m1")


B, L_IMG, L_TXT, DM, H, D = 1, 768, 256, 1024, 8, 128
L = L_TXT + L_IMG
HD = H * D
EPS = 1e-6


def rms(x, gain):
    return x / np.sqrt(np.mean(np.square(x), axis=-1, keepdims=True) + EPS) * gain


def qkv(x, w, qn, kn):
    y = (mxq(x, 2, "e4m3") @ w).reshape(x.shape[0], x.shape[1], 3, H, D)
    return rms(y[:, :, 0], qn), rms(y[:, :, 1], kn), y[:, :, 2]


def rope(x, fc):
    x_ = x.reshape(x.shape[:-1] + (D // 2, 1, 2))
    out = fc[:, None, :, :, 0] * x_[..., 0] + fc[:, None, :, :, 1] * x_[..., 1]
    return out.reshape(x.shape)


def setup_inputs():
    s = mx_kscale(DM)
    r = np.random.standard_normal
    hidden_states = bf(r((B, L_IMG, DM)) * s)
    encoder_hidden_states = bf(r((B, L_TXT, DM)) * s)
    image_rotary_emb = bf(r((L, D // 2, 4)) * 0.6)
    iqkv_words, iqkv_scales = pack4(r((DM, 3 * HD)) / np.sqrt(DM) / s[:, None])
    eqkv_words, eqkv_scales = pack4(r((DM, 3 * HD)) / np.sqrt(DM) / s[:, None])
    return {
        "hidden_states": hidden_states,
        "encoder_hidden_states": encoder_hidden_states,
        "image_rotary_emb": image_rotary_emb,
        "W_iqkv_words": iqkv_words,
        "W_iqkv_scales": iqkv_scales,
        "W_eqkv_words": eqkv_words,
        "W_eqkv_scales": eqkv_scales,
        "qn_scale": bf(1.0 + 0.1 * r(D)),
        "kn_scale": bf(1.0 + 0.1 * r(D)),
        "eqn_scale": bf(1.0 + 0.1 * r(D)),
        "ekn_scale": bf(1.0 + 0.1 * r(D)),
    }


def reference(hidden_states, encoder_hidden_states, image_rotary_emb, W_iqkv_words, W_iqkv_scales, W_eqkv_words, W_eqkv_scales, qn_scale, kn_scale, eqn_scale, ekn_scale):
    q, k, v = qkv(f64(hidden_states), unpack4(W_iqkv_words, W_iqkv_scales), f64(qn_scale), f64(kn_scale))
    eq, ek, ev = qkv(f64(encoder_hidden_states), unpack4(W_eqkv_words, W_eqkv_scales), f64(eqn_scale), f64(ekn_scale))
    q = np.concatenate((eq, q), axis=1)
    k = np.concatenate((ek, k), axis=1)
    v = np.concatenate((ev, v), axis=1)
    fc = f64(image_rotary_emb).reshape(L, D // 2, 2, 2)
    return rope(q, fc).reshape(B, L, HD), rope(k, fc).reshape(B, L, HD), v.reshape(B, L, HD)

@@ -1,0 +1,248 @@
+from contextlib import ExitStack
+
+import concourse.mybir as mybir
+from concourse.masks import make_identity
+
+F32 = mybir.dt.float32
+BF16 = mybir.dt.bfloat16
+I32 = mybir.dt.int32
+U32 = mybir.dt.uint32
+U8 = mybir.dt.uint8
+FP8X4 = mybir.dt.float8_e4m3fn_x4
+FP4X4 = mybir.dt.float4_e2m1fn_x4
+ACT = mybir.ActivationFunctionType
+ALU = mybir.AluOpType
+
+P = 128
+PACK = 4
+DM = 1024
+PASSES = DM // (P * PACK)
+HEADS = 8
+D = 128
+HD = HEADS * D
+BANK = 512
+HEADS_PER_BANK = BANK // D
+Q, K, V = 0, 1, 2
+EPS = 1e-6
+
+FLOPS = 2 * 1024 * DM * 3 * HD
+
+
+def tile_fluxattention_pa_kernel(
+    tc,
+    hidden_states,
+    encoder_hidden_states,
+    image_rotary_emb,
+    W_iqkv_words,
+    W_iqkv_scales,
+    W_eqkv_words,
+    W_eqkv_scales,
+    qn_scale,
+    kn_scale,
+    eqn_scale,
+    ekn_scale,
+    out_0,
+    out_1,
+    out_2,
+):
+    nc = tc.nc
+
+    text = {
+        "name": "text",
+        "x": encoder_hidden_states.flatten_outer_dims(),
+        "words": W_eqkv_words,
+        "scales": W_eqkv_scales,
+        "first": 0,
+        "tiles": 2,
+        "gain_slot": 0,
+    }
+    image = {
+        "name": "image",
+        "x": hidden_states.flatten_outer_dims(),
+        "words": W_iqkv_words,
+        "scales": W_iqkv_scales,
+        "first": 256,
+        "tiles": 6,
+        "gain_slot": 2,
+    }
+    gains = (eqn_scale, ekn_scale, qn_scale, kn_scale)
+    token_tiles = [(stream, t) for stream in (text, image) for t in range(stream["tiles"])]
+
+    def by_tile(rows, stream):
+        return rows.rearrange("(p t) w -> p t w", t=stream["tiles"])
+
+    def positions(rows, stream):
+        return by_tile(rows[stream["first"] : stream["first"] + P * stream["tiles"], :], stream)
+
+    with ExitStack() as ctx:
+        keep = ctx.enter_context(tc.tile_pool(name="keep", bufs=1))
+        stage = ctx.enter_context(tc.tile_pool(name="stage", bufs=2))
+        quantised = ctx.enter_context(tc.tile_pool(name="quantised", bufs=3))
+        stats = ctx.enter_context(tc.tile_pool(name="stats", bufs=4))
+        squares = ctx.enter_context(tc.tile_pool(name="squares", bufs=2))
+        results = ctx.enter_context(tc.tile_pool(name="results", bufs=4))
+        psum_turn = ctx.enter_context(tc.psum_pool(name="psum_turn", bufs=1))
+        psum_acc = ctx.enter_context(tc.psum_pool(name="psum_acc", bufs=7))
+        ctx.enter_context(tc.manual_schedule())
+
+        gain_rows = keep.tile([P, 4 * D], BF16)
+        nc.vector.memset(gain_rows[:], 0.0)
+        for slot, gain in enumerate(gains):
+            nc.scalar.dma_start(out=gain_rows[0:1, slot * D : (slot + 1) * D], in_=gain.unsqueeze(0))
+
+        identity = keep.tile([P, P], F32)
+        make_identity(nc, identity[:])
+        ones = keep.tile([P, P], BF16)
+        eps = keep.tile([P, 1], F32)
+
+        for stream in (text, image):
+            stream["planes"] = keep.tile([P, PASSES, 3 * HD], U8, name="planes_%s" % stream["name"], align_bytes=64)
+            nc.vector.memset(stream["planes"][:].bitcast(I32), 0)
+            if stream is text:
+                nc.vector.memset(ones[:], 1.0)
+                nc.vector.memset(eps[:], EPS)
+
+        def load_x(stream, pair):
+            x_sb = keep.tile([P, 2, DM], BF16, name="x_%s_%d" % (stream["name"], pair))
+            nc.sync.dma_start(out=x_sb[:], in_=by_tile(stream["x"], stream)[:, 2 * pair : 2 * pair + 2, :])
+            stream["x_sb"].append(x_sb)
+
+        def load_words(stream, part):
+            words = keep.tile([P, PASSES, 2 * HD], U8, name="words_%s_%d" % (stream["name"], part), align_bytes=64)
+            source = stream["words"].bitcast(I32)[:, :, part * HD // 2 : (part + 1) * HD // 2]
+            nc.sync.dma_start(out=words[:].bitcast(I32), in_=source.rearrange("g p w -> p g w"))
+            stream["words_sb"][part] = words
+
+        def load_scales(stream):
+            source = stream["scales"].bitcast(I32)
+            for quadrant in range(4):
+                nc.sync.dma_start(
+                    out=stream["planes"][32 * quadrant : 32 * quadrant + 4, :, :].bitcast(I32),
+                    in_=source[:, 4 * quadrant : 4 * quadrant + 4, :].rearrange("g r n -> r g n"),
+                )
+
+        def load_rotary(stream):
+            rotary = keep.tile([P, stream["tiles"], 2 * D], BF16, name="rotary_%s" % stream["name"])
+            nc.sync.dma_start(out=rotary[:], in_=positions(image_rotary_emb.rearrange("l i c -> l (i c)"), stream))
+            stream["rotary"] = rotary
+
+        for stream in (text, image):
+            stream["x_sb"] = []
+            stream["words_sb"] = {}
+        load_x(text, 0)
+        load_words(text, Q)
+        load_scales(text)
+        load_rotary(text)
+        load_rotary(image)
+        load_words(text, V)
+        load_words(text, K)
+        load_x(image, 0)
+        load_scales(image)
+        load_words(image, Q)
+        load_words(image, V)
+        load_words(image, K)
+        load_x(image, 1)
+        load_x(image, 2)
+
+        warm = keep.tile([P, 1], F32)
+        nc.scalar.activation(out=warm[:], in_=eps[:], func=ACT.Abs_reciprocal_sqrt)
+
+        gain_bank = psum_acc.tile([P, BANK], F32, tag="acc")
+        nc.tensor.matmul(out=gain_bank[:], lhsT=ones[:], rhs=gain_rows[:], start=True, stop=True)
+        gain_all = keep.tile([P, 4, D], F32)
+        nc.scalar.copy(out=gain_all[:].rearrange("p s f -> p (s f)"), in_=gain_bank[:])
+
+        def quantise_tokens(n):
+            stream, t = token_tiles[n]
+            x_words = stream["x_sb"][t // 2][:, t % 2, :].bitcast(F32)
+            turned = psum_turn.tile([P, PASSES, 2, P], F32)
+            for g in range(PASSES):
+                for u in range(2):
+                    nc.tensor.transpose(turned[:, g, u, :], x_words[:, 256 * g + u : 256 * (g + 1) : 2], identity[:])
+            grouped = stage.tile([P, PASSES * P * PACK], BF16, align_bytes=64)
+            nc.scalar.copy(
+                out=grouped[:].bitcast(F32).rearrange("p (g r u) -> p g r u", g=PASSES, u=2),
+                in_=turned[:].rearrange("p g u r -> p g r u"),
+            )
+            x_codes = quantised.tile([P, PASSES * P], U32, align_bytes=64)
+            x_scales = quantised.tile([P, PASSES * P], U8, align_bytes=64)
+            nc.vector.quantize_mx(out=x_codes[:].bitcast(FP8X4), scales=x_scales[:], in_=grouped[:])
+            return x_codes, x_scales
+
+        def make_tables(n):
+            stream, t = token_tiles[n]
+            table = keep.tile([P, 2, 2, D], F32, name="table_%d" % n)
+            matrices = stream["rotary"][:, t, :].rearrange("p (i a b) -> p b i a", a=2, b=2)
+            for part in (Q, K):
+                gain = gain_all[:, stream["gain_slot"] + part, :].rearrange("p (i b) -> p b i", b=2)
+                nc.vector.tensor_tensor(
+                    out=table[:, part, :, :].rearrange("p b (i a) -> p b i a", a=2),
+                    in0=matrices,
+                    in1=gain.unsqueeze(3).to_broadcast([P, 2, D // 2, 2]),
+                    op=ALU.mult,
+                )
+            return table
+
+        def project(stream, x_codes, x_scales, part, half):
+            acc = psum_acc.tile([P, BANK], F32, tag="acc")
+            for g in range(PASSES):
+                nc.tensor.matmul_mx(
+                    out=acc[:],
+                    lhsT=x_codes[:, g * P : (g + 1) * P].bitcast(FP8X4),
+                    lhsT_scale=x_scales[:, g * P : (g + 1) * P],
+                    rhs=stream["words_sb"][part][:, g, 2 * BANK * half : 2 * BANK * (half + 1)].bitcast(FP4X4),
+                    rhs_scale=stream["planes"][:, g, part * HD + BANK * half : part * HD + BANK * (half + 1)],
+                    start=(g == 0),
+                    stop=(g == PASSES - 1),
+                )
+            return acc
+
+        operands = quantise_tokens(0)
+        tables = [make_tables(n) for n in range(len(token_tiles))]
+
+        for n, (stream, t) in enumerate(token_tiles):
+            x_codes, x_scales = operands
+            v_sb = results.tile([P, HD], F32)
+            for step, part in enumerate((Q, K)):
+                banks = []
+                sum_sq = stats.tile([P, HEADS], F32)
+                unused = squares.tile([P, HEADS, D], BF16)
+                for half in range(2):
+                    acc = project(stream, x_codes, x_scales, part, half)
+                    banks.append(acc)
+                    for j in range(HEADS_PER_BANK):
+                        h = HEADS_PER_BANK * half + j
+                        nc.scalar.activation(
+                            out=unused[:, h, :],
+                            in_=acc[:, j * D : (j + 1) * D],
+                            func=ACT.Square,
+                            accum_out=sum_sq[:, h : h + 1],
+                        )
+                v_acc = project(stream, x_codes, x_scales, V, step)
+                nc.scalar.copy(out=v_sb[:, step * BANK : (step + 1) * BANK], in_=v_acc[:])
+                norm = stats.tile([P, HEADS], F32)
+                nc.scalar.activation(
+                    out=norm[:], in_=sum_sq[:], func=ACT.Abs_reciprocal_sqrt, bias=eps[:], scale=1.0 / D
+                )
+
+                if step == 0 and n + 1 < len(token_tiles):
+                    operands = quantise_tokens(n + 1)
+                if step == 1:
+                    nc.sync.dma_start(out=positions(out_2.flatten_outer_dims(), stream)[:, t, :], in_=v_sb[:])
+
+                terms = (results.tile([P, HD], F32, name="term_0"), results.tile([P, HD], F32, name="term_1"))
+                for h in range(HEADS):
+                    j = h % HEADS_PER_BANK
+                    x_pairs = banks[h // HEADS_PER_BANK][:, j * D : (j + 1) * D].rearrange("p (i b) -> p i b", b=2)
+                    for b in range(2):
+                        nc.vector.scalar_tensor_tensor(
+                            out=terms[b][:, h * D : (h + 1) * D].rearrange("p (i a) -> p i a", a=2),
+                            in0=x_pairs[:, :, b : b + 1].to_broadcast([P, D // 2, 2]),
+                            scalar=norm[:, h : h + 1],
+                            in1=tables[n][:, part, b, :].rearrange("p (i a) -> p i a", a=2),
+                            op0=ALU.mult,
+                            op1=ALU.mult,
+                        )
+                nc.gpsimd.tensor_tensor(out=terms[0][:], in0=terms[0][:], in1=terms[1][:], op=ALU.add)
+                out_part = (out_0, out_1)[part]
+                nc.sync.dma_start(out=positions(out_part.flatten_outer_dims(), stream)[:, t, :], in_=terms[0][:])

@@ -24,6 +24,8 @@ BANK = 512
 HEADS_PER_BANK = BANK // D
 Q, K, V = 0, 1, 2
 EPS = 1e-6
+WARM_UP = 8
+VECTOR_TABLES = 5
 
 FLOPS = 2 * 1024 * DM * 3 * HD
 
@@ -81,37 +83,43 @@ def tile_fluxattention_pa_kernel(
         stats = ctx.enter_context(tc.tile_pool(name="stats", bufs=4))
         squares = ctx.enter_context(tc.tile_pool(name="squares", bufs=2))
         results = ctx.enter_context(tc.tile_pool(name="results", bufs=4))
-        psum_turn = ctx.enter_context(tc.psum_pool(name="psum_turn", bufs=1))
-        psum_acc = ctx.enter_context(tc.psum_pool(name="psum_acc", bufs=7))
+        psum = ctx.enter_context(tc.psum_pool(name="psum", bufs=8))
         ctx.enter_context(tc.manual_schedule())
 
         gain_rows = keep.tile([P, 4 * D], BF16)
-        nc.vector.memset(gain_rows[:], 0.0)
+        nc.gpsimd.memset(gain_rows[:], 0.0)
         for slot, gain in enumerate(gains):
             nc.scalar.dma_start(out=gain_rows[0:1, slot * D : (slot + 1) * D], in_=gain.unsqueeze(0))
+        ones = keep.tile([P, P], BF16)
+        nc.vector.memset(ones[:], 1.0)
+        eps = keep.tile([P, 1], F32)
+        nc.vector.memset(eps[:], EPS)
 
         identity = keep.tile([P, P], F32)
         make_identity(nc, identity[:])
-        ones = keep.tile([P, P], BF16)
-        eps = keep.tile([P, 1], F32)
 
         for stream in (text, image):
             stream["planes"] = keep.tile([P, PASSES, 3 * HD], U8, name="planes_%s" % stream["name"], align_bytes=64)
             nc.vector.memset(stream["planes"][:].bitcast(I32), 0)
-            if stream is text:
-                nc.vector.memset(ones[:], 1.0)
-                nc.vector.memset(eps[:], EPS)
+            stream["x_sb"] = {}
+            stream["words_sb"] = {}
 
-        def load_x(stream, pair):
-            x_sb = keep.tile([P, 2, DM], BF16, name="x_%s_%d" % (stream["name"], pair))
-            nc.sync.dma_start(out=x_sb[:], in_=by_tile(stream["x"], stream)[:, 2 * pair : 2 * pair + 2, :])
-            stream["x_sb"].append(x_sb)
+        def load_x(stream, first, count):
+            x_sb = keep.tile([P, count, DM], BF16, name="x_%s_%d" % (stream["name"], first))
+            nc.sync.dma_start(out=x_sb[:], in_=by_tile(stream["x"], stream)[:, first : first + count, :])
+            for j in range(count):
+                stream["x_sb"][first + j] = x_sb[:, j, :]
 
-        def load_words(stream, part):
-            words = keep.tile([P, PASSES, 2 * HD], U8, name="words_%s_%d" % (stream["name"], part), align_bytes=64)
-            source = stream["words"].bitcast(I32)[:, :, part * HD // 2 : (part + 1) * HD // 2]
+        def load_words(stream, part, halves):
+            width = len(halves) * BANK
+            words = keep.tile(
+                [P, PASSES, 2 * width], U8, name="words_%s_%d_%d" % (stream["name"], part, halves[0]), align_bytes=64
+            )
+            start = (part * HD + halves[0] * BANK) // 2
+            source = stream["words"].bitcast(I32)[:, :, start : start + width // 2]
             nc.sync.dma_start(out=words[:].bitcast(I32), in_=source.rearrange("g p w -> p g w"))
-            stream["words_sb"][part] = words
+            for j, half in enumerate(halves):
+                stream["words_sb"][(part, half)] = words[:, :, 2 * BANK * j : 2 * BANK * (j + 1)]
 
         def load_scales(stream):
             source = stream["scales"].bitcast(I32)
@@ -126,56 +134,68 @@ def tile_fluxattention_pa_kernel(
             nc.sync.dma_start(out=rotary[:], in_=positions(image_rotary_emb.rearrange("l i c -> l (i c)"), stream))
             stream["rotary"] = rotary
 
-        for stream in (text, image):
-            stream["x_sb"] = []
-            stream["words_sb"] = {}
-        load_x(text, 0)
-        load_words(text, Q)
+        load_x(text, 0, 1)
+        load_words(text, Q, (0, 1))
         load_scales(text)
         load_rotary(text)
         load_rotary(image)
-        load_words(text, V)
-        load_words(text, K)
-        load_x(image, 0)
+        load_words(text, K, (0, 1))
+        load_x(text, 1, 1)
+        load_words(text, V, (0, 1))
+        load_x(image, 0, 2)
         load_scales(image)
-        load_words(image, Q)
-        load_words(image, V)
-        load_words(image, K)
-        load_x(image, 1)
-        load_x(image, 2)
+        load_words(image, Q, (0, 1))
+        load_words(image, K, (0, 1))
+        load_words(image, V, (0, 1))
+        load_x(image, 2, 2)
+        load_x(image, 4, 2)
 
         warm = keep.tile([P, 1], F32)
         nc.scalar.activation(out=warm[:], in_=eps[:], func=ACT.Abs_reciprocal_sqrt)
 
-        gain_bank = psum_acc.tile([P, BANK], F32, tag="acc")
-        nc.tensor.matmul(out=gain_bank[:], lhsT=ones[:], rhs=gain_rows[:], start=True, stop=True)
-        gain_all = keep.tile([P, 4, D], F32)
-        nc.scalar.copy(out=gain_all[:].rearrange("p s f -> p (s f)"), in_=gain_bank[:])
+        warm_bank = psum.tile([P, BANK], F32, tag="bank")
 
-        def quantise_tokens(n):
+        def warm_up(count):
+            for i in range(count):
+                nc.tensor.matmul(out=warm_bank[:, 0:P], lhsT=ones[:], rhs=ones[:], start=True, stop=True)
+
+        warm_up(WARM_UP)
+
+        def turn(n):
             stream, t = token_tiles[n]
-            x_words = stream["x_sb"][t // 2][:, t % 2, :].bitcast(F32)
-            turned = psum_turn.tile([P, PASSES, 2, P], F32)
+            x_words = stream["x_sb"][t].bitcast(F32)
+            turned = psum.tile([P, BANK], F32, tag="bank")
             for g in range(PASSES):
                 for u in range(2):
-                    nc.tensor.transpose(turned[:, g, u, :], x_words[:, 256 * g + u : 256 * (g + 1) : 2], identity[:])
+                    nc.tensor.transpose(
+                        turned[:, (2 * g + u) * P : (2 * g + u + 1) * P],
+                        x_words[:, 256 * g + u : 256 * (g + 1) : 2],
+                        identity[:],
+                    )
+            return turned
+
+        def group(turned):
             grouped = stage.tile([P, PASSES * P * PACK], BF16, align_bytes=64)
             nc.scalar.copy(
                 out=grouped[:].bitcast(F32).rearrange("p (g r u) -> p g r u", g=PASSES, u=2),
-                in_=turned[:].rearrange("p g u r -> p g r u"),
+                in_=turned[:].rearrange("p (g u r) -> p g r u", g=PASSES, u=2),
             )
+            return grouped
+
+        def quantise(grouped):
             x_codes = quantised.tile([P, PASSES * P], U32, align_bytes=64)
             x_scales = quantised.tile([P, PASSES * P], U8, align_bytes=64)
             nc.vector.quantize_mx(out=x_codes[:].bitcast(FP8X4), scales=x_scales[:], in_=grouped[:])
             return x_codes, x_scales
 
-        def make_tables(n):
+        def make_tables(n, engine, gain_source):
             stream, t = token_tiles[n]
             table = keep.tile([P, 2, 2, D], F32, name="table_%d" % n)
             matrices = stream["rotary"][:, t, :].rearrange("p (i a b) -> p b i a", a=2, b=2)
             for part in (Q, K):
-                gain = gain_all[:, stream["gain_slot"] + part, :].rearrange("p (i b) -> p b i", b=2)
-                nc.vector.tensor_tensor(
+                slot = stream["gain_slot"] + part
+                gain = gain_source[:, slot * D : (slot + 1) * D].rearrange("p (i b) -> p b i", b=2)
+                engine.tensor_tensor(
                     out=table[:, part, :, :].rearrange("p b (i a) -> p b i a", a=2),
                     in0=matrices,
                     in1=gain.unsqueeze(3).to_broadcast([P, 2, D // 2, 2]),
@@ -183,32 +203,85 @@ def tile_fluxattention_pa_kernel(
                 )
             return table
 
-        def project(stream, x_codes, x_scales, part, half):
-            acc = psum_acc.tile([P, BANK], F32, tag="acc")
+        def project(n, operands, part, half):
+            stream = token_tiles[n][0]
+            x_codes, x_scales = operands
+            acc = psum.tile([P, BANK], F32, tag="bank")
             for g in range(PASSES):
                 nc.tensor.matmul_mx(
                     out=acc[:],
                     lhsT=x_codes[:, g * P : (g + 1) * P].bitcast(FP8X4),
                     lhsT_scale=x_scales[:, g * P : (g + 1) * P],
-                    rhs=stream["words_sb"][part][:, g, 2 * BANK * half : 2 * BANK * (half + 1)].bitcast(FP4X4),
+                    rhs=stream["words_sb"][(part, half)][:, g, :].bitcast(FP4X4),
                     rhs_scale=stream["planes"][:, g, part * HD + BANK * half : part * HD + BANK * (half + 1)],
                     start=(g == 0),
                     stop=(g == PASSES - 1),
                 )
             return acc
 
-        operands = quantise_tokens(0)
-        tables = [make_tables(n) for n in range(len(token_tiles))]
+        def root(norm, sum_sq, heads):
+            nc.scalar.activation(
+                out=norm[:, heads], in_=sum_sq[:, heads], func=ACT.Abs_reciprocal_sqrt, bias=eps[:], scale=1.0 / D
+            )
 
-        for n, (stream, t) in enumerate(token_tiles):
-            x_codes, x_scales = operands
-            v_sb = results.tile([P, HD], F32)
+        def products(n, part, banks, norm, terms, heads):
+            for h in heads:
+                j = h % HEADS_PER_BANK
+                x_pairs = banks[h // HEADS_PER_BANK][:, j * D : (j + 1) * D].rearrange("p (i b) -> p i b", b=2)
+                for b in range(2):
+                    nc.vector.scalar_tensor_tensor(
+                        out=terms[b][:, h * D : (h + 1) * D].rearrange("p (i a) -> p i a", a=2),
+                        in0=x_pairs[:, :, b : b + 1].to_broadcast([P, D // 2, 2]),
+                        scalar=norm[:, h : h + 1],
+                        in1=tables[n][:, part, b, :].rearrange("p (i a) -> p i a", a=2),
+                        op0=ALU.mult,
+                        op1=ALU.mult,
+                    )
+
+        def add_and_store(n, part, terms, columns):
+            stream, t = token_tiles[n]
+            nc.gpsimd.tensor_tensor(out=terms[0][:, columns], in0=terms[0][:, columns], in1=terms[1][:, columns], op=ALU.add)
+            out_part = (out_0, out_1)[part]
+            nc.sync.dma_start(out=positions(out_part.flatten_outer_dims(), stream)[:, t, columns], in_=terms[0][:, columns])
+
+        v_tiles = {}
+
+        def value(unit):
+            n, half = unit // 2, unit % 2
+            stream, t = token_tiles[n]
+            if half == 0:
+                v_sb = results.tile([P, HD], F32, name="v_sb")
+                v_tiles[n] = v_sb
+            v_acc = project(n, operands[n], V, half)
+            nc.scalar.copy(out=v_tiles[n][:, half * BANK : (half + 1) * BANK], in_=v_acc[:])
+            if half == 1:
+                nc.sync.dma_start(out=positions(out_2.flatten_outer_dims(), stream)[:, t, :], in_=v_tiles[n][:])
+
+        tiles = len(token_tiles)
+        operands = {}
+        tables = {}
+        grouped = group(turn(0))
+        gain_bank = psum.tile([P, BANK], F32, tag="bank")
+        nc.tensor.matmul(out=gain_bank[:], lhsT=ones[:], rhs=gain_rows[:], start=True, stop=True)
+        warm_up(WARM_UP)
+        operands[0] = quantise(grouped)
+        gain_all = keep.tile([P, 4 * D], F32)
+        nc.scalar.copy(out=gain_all[:], in_=gain_bank[:])
+        for m in range(VECTOR_TABLES):
+            tables[m] = make_tables(m, nc.vector, gain_bank)
+        for m in range(VECTOR_TABLES, tiles):
+            tables[m] = make_tables(m, nc.gpsimd, gain_all)
+
+        for n in range(tiles):
             for step, part in enumerate((Q, K)):
+                s = 2 * n + step
+                fine = s == 0 or s == 2 * tiles - 1
                 banks = []
                 sum_sq = stats.tile([P, HEADS], F32)
+                norm = stats.tile([P, HEADS], F32)
                 unused = squares.tile([P, HEADS, D], BF16)
                 for half in range(2):
-                    acc = project(stream, x_codes, x_scales, part, half)
+                    acc = project(n, operands[n], part, half)
                     banks.append(acc)
                     for j in range(HEADS_PER_BANK):
                         h = HEADS_PER_BANK * half + j
@@ -218,31 +291,29 @@ def tile_fluxattention_pa_kernel(
                             func=ACT.Square,
                             accum_out=sum_sq[:, h : h + 1],
                         )
-                v_acc = project(stream, x_codes, x_scales, V, step)
-                nc.scalar.copy(out=v_sb[:, step * BANK : (step + 1) * BANK], in_=v_acc[:])
-                norm = stats.tile([P, HEADS], F32)
-                nc.scalar.activation(
-                    out=norm[:], in_=sum_sq[:], func=ACT.Abs_reciprocal_sqrt, bias=eps[:], scale=1.0 / D
-                )
+                    if s == 0:
+                        root(norm, sum_sq, slice(HEADS_PER_BANK * half, HEADS_PER_BANK * (half + 1)))
+                if s == 1:
+                    root(norm, sum_sq, slice(0, HEADS))
+                if s >= 1:
+                    value(s - 1)
+                if s >= 2:
+                    root(norm, sum_sq, slice(0, HEADS))
+                if s == 2 * tiles - 1:
+                    value(s)
 
-                if step == 0 and n + 1 < len(token_tiles):
-                    operands = quantise_tokens(n + 1)
-                if step == 1:
-                    nc.sync.dma_start(out=positions(out_2.flatten_outer_dims(), stream)[:, t, :], in_=v_sb[:])
+                if step == 0 and n + 1 < tiles:
+                    grouped = group(turn(n + 1))
+                    if n > 0:
+                        operands[n + 1] = quantise(grouped)
 
                 terms = (results.tile([P, HD], F32, name="term_0"), results.tile([P, HD], F32, name="term_1"))
-                for h in range(HEADS):
-                    j = h % HEADS_PER_BANK
-                    x_pairs = banks[h // HEADS_PER_BANK][:, j * D : (j + 1) * D].rearrange("p (i b) -> p i b", b=2)
-                    for b in range(2):
-                        nc.vector.scalar_tensor_tensor(
-                            out=terms[b][:, h * D : (h + 1) * D].rearrange("p (i a) -> p i a", a=2),
-                            in0=x_pairs[:, :, b : b + 1].to_broadcast([P, D // 2, 2]),
-                            scalar=norm[:, h : h + 1],
-                            in1=tables[n][:, part, b, :].rearrange("p (i a) -> p i a", a=2),
-                            op0=ALU.mult,
-                            op1=ALU.mult,
-                        )
-                nc.gpsimd.tensor_tensor(out=terms[0][:], in0=terms[0][:], in1=terms[1][:], op=ALU.add)
-                out_part = (out_0, out_1)[part]
-                nc.sync.dma_start(out=positions(out_part.flatten_outer_dims(), stream)[:, t, :], in_=terms[0][:])
+                if fine:
+                    for half in range(2):
+                        products(n, part, banks, norm, terms, range(HEADS_PER_BANK * half, HEADS_PER_BANK * (half + 1)))
+                        if s == 0 and half == 0:
+                            operands[1] = quantise(grouped)
+                        add_and_store(n, part, terms, slice(BANK * half, BANK * (half + 1)))
+                else:
+                    products(n, part, banks, norm, terms, range(HEADS))
+                    add_and_store(n, part, terms, slice(0, HD))

@@ -25,7 +25,7 @@ HEADS_PER_BANK = BANK // D
 Q, K, V = 0, 1, 2
 EPS = 1e-6
 WARM_UP = 8
-VECTOR_TABLES = 5
+VECTOR_TABLES = 8
 
 FLOPS = 2 * 1024 * DM * 3 * HD
 

@@ -24,7 +24,6 @@ BANK = 512
 HEADS_PER_BANK = BANK // D
 Q, K, V = 0, 1, 2
 EPS = 1e-6
-WARM_UP = 8
 VECTOR_TABLES = 8
 
 FLOPS = 2 * 1024 * DM * 3 * HD
@@ -87,7 +86,7 @@ def tile_fluxattention_pa_kernel(
         ctx.enter_context(tc.manual_schedule())
 
         gain_rows = keep.tile([P, 4 * D], BF16)
-        nc.gpsimd.memset(gain_rows[:], 0.0)
+        nc.vector.memset(gain_rows[:], 0.0)
         for slot, gain in enumerate(gains):
             nc.scalar.dma_start(out=gain_rows[0:1, slot * D : (slot + 1) * D], in_=gain.unsqueeze(0))
         ones = keep.tile([P, P], BF16)
@@ -134,32 +133,28 @@ def tile_fluxattention_pa_kernel(
             nc.sync.dma_start(out=rotary[:], in_=positions(image_rotary_emb.rearrange("l i c -> l (i c)"), stream))
             stream["rotary"] = rotary
 
-        load_x(text, 0, 1)
+        load_x(text, 0, 2)
         load_words(text, Q, (0, 1))
         load_scales(text)
         load_rotary(text)
         load_rotary(image)
-        load_words(text, K, (0, 1))
-        load_x(text, 1, 1)
         load_words(text, V, (0, 1))
+        load_words(text, K, (0, 1))
         load_x(image, 0, 2)
         load_scales(image)
         load_words(image, Q, (0, 1))
-        load_words(image, K, (0, 1))
         load_words(image, V, (0, 1))
+        load_words(image, K, (0, 1))
         load_x(image, 2, 2)
         load_x(image, 4, 2)
 
         warm = keep.tile([P, 1], F32)
         nc.scalar.activation(out=warm[:], in_=eps[:], func=ACT.Abs_reciprocal_sqrt)
 
-        warm_bank = psum.tile([P, BANK], F32, tag="bank")
-
-        def warm_up(count):
-            for i in range(count):
-                nc.tensor.matmul(out=warm_bank[:, 0:P], lhsT=ones[:], rhs=ones[:], start=True, stop=True)
-
-        warm_up(WARM_UP)
+        gain_bank = psum.tile([P, BANK], F32, tag="bank")
+        nc.tensor.matmul(out=gain_bank[:], lhsT=ones[:], rhs=gain_rows[:], start=True, stop=True)
+        gain_all = keep.tile([P, 4 * D], F32)
+        nc.scalar.copy(out=gain_all[:], in_=gain_bank[:])
 
         def turn(n):
             stream, t = token_tiles[n]
@@ -261,14 +256,9 @@ def tile_fluxattention_pa_kernel(
         operands = {}
         tables = {}
         grouped = group(turn(0))
-        gain_bank = psum.tile([P, BANK], F32, tag="bank")
-        nc.tensor.matmul(out=gain_bank[:], lhsT=ones[:], rhs=gain_rows[:], start=True, stop=True)
-        warm_up(WARM_UP)
         operands[0] = quantise(grouped)
-        gain_all = keep.tile([P, 4 * D], F32)
-        nc.scalar.copy(out=gain_all[:], in_=gain_bank[:])
         for m in range(VECTOR_TABLES):
-            tables[m] = make_tables(m, nc.vector, gain_bank)
+            tables[m] = make_tables(m, nc.vector, gain_all)
         for m in range(VECTOR_TABLES, tiles):
             tables[m] = make_tables(m, nc.gpsimd, gain_all)
 

@@ -265,7 +265,7 @@ def tile_fluxattention_pa_kernel(
         for n in range(tiles):
             for step, part in enumerate((Q, K)):
                 s = 2 * n + step
-                fine = s == 0 or s == 2 * tiles - 1
+                fine = False
                 banks = []
                 sum_sq = stats.tile([P, HEADS], F32)
                 norm = stats.tile([P, HEADS], F32)
@@ -281,21 +281,15 @@ def tile_fluxattention_pa_kernel(
                             func=ACT.Square,
                             accum_out=sum_sq[:, h : h + 1],
                         )
-                    if s == 0:
-                        root(norm, sum_sq, slice(HEADS_PER_BANK * half, HEADS_PER_BANK * (half + 1)))
-                if s == 1:
-                    root(norm, sum_sq, slice(0, HEADS))
                 if s >= 1:
                     value(s - 1)
-                if s >= 2:
-                    root(norm, sum_sq, slice(0, HEADS))
+                root(norm, sum_sq, slice(0, HEADS))
                 if s == 2 * tiles - 1:
                     value(s)
 
                 if step == 0 and n + 1 < tiles:
                     grouped = group(turn(n + 1))
-                    if n > 0:
-                        operands[n + 1] = quantise(grouped)
+                    operands[n + 1] = quantise(grouped)
 
                 terms = (results.tile([P, HD], F32, name="term_0"), results.tile([P, HD], F32, name="term_1"))
                 if fine:

@@ -185,15 +185,15 @@ def tile_fluxattention_pa_kernel(
 
         def make_tables(n, engine, gain_source):
             stream, t = token_tiles[n]
-            table = keep.tile([P, 2, 2, D], F32, name="table_%d" % n)
-            matrices = stream["rotary"][:, t, :].rearrange("p (i a b) -> p b i a", a=2, b=2)
+            table = keep.tile([P, 2, 2 * D], F32, name="table_%d" % n)
+            matrices = stream["rotary"][:, t, :].rearrange("p (i a b) -> p i b a", a=2, b=2)
             for part in (Q, K):
                 slot = stream["gain_slot"] + part
-                gain = gain_source[:, slot * D : (slot + 1) * D].rearrange("p (i b) -> p b i", b=2)
+                gain = gain_source[:, slot * D : (slot + 1) * D].rearrange("p (i b) -> p i b", b=2)
                 engine.tensor_tensor(
-                    out=table[:, part, :, :].rearrange("p b (i a) -> p b i a", a=2),
+                    out=table[:, part, :].rearrange("p (i b a) -> p i b a", a=2, b=2),
                     in0=matrices,
-                    in1=gain.unsqueeze(3).to_broadcast([P, 2, D // 2, 2]),
+                    in1=gain.unsqueeze(3).to_broadcast([P, D // 2, 2, 2]),
                     op=ALU.mult,
                 )
             return table
@@ -222,22 +222,24 @@ def tile_fluxattention_pa_kernel(
         def products(n, part, banks, norm, terms, heads):
             for h in heads:
                 j = h % HEADS_PER_BANK
-                x_pairs = banks[h // HEADS_PER_BANK][:, j * D : (j + 1) * D].rearrange("p (i b) -> p i b", b=2)
-                for b in range(2):
-                    nc.vector.scalar_tensor_tensor(
-                        out=terms[b][:, h * D : (h + 1) * D].rearrange("p (i a) -> p i a", a=2),
-                        in0=x_pairs[:, :, b : b + 1].to_broadcast([P, D // 2, 2]),
-                        scalar=norm[:, h : h + 1],
-                        in1=tables[n][:, part, b, :].rearrange("p (i a) -> p i a", a=2),
-                        op0=ALU.mult,
-                        op1=ALU.mult,
-                    )
+                nc.vector.scalar_tensor_tensor(
+                    out=terms[:, 2 * h * D : 2 * (h + 1) * D].rearrange("p (f a) -> p f a", a=2),
+                    in0=banks[h // HEADS_PER_BANK][:, j * D : (j + 1) * D].unsqueeze(2).to_broadcast([P, D, 2]),
+                    scalar=norm[:, h : h + 1],
+                    in1=tables[n][:, part, :].rearrange("p (f a) -> p f a", a=2),
+                    op0=ALU.mult,
+                    op1=ALU.mult,
+                )
 
-        def add_and_store(n, part, terms, columns):
+        def add_and_store(n, part, terms):
             stream, t = token_tiles[n]
-            nc.gpsimd.tensor_tensor(out=terms[0][:, columns], in0=terms[0][:, columns], in1=terms[1][:, columns], op=ALU.add)
+            pairs = terms[:].rearrange("p (m b a) -> p m b a", a=2, b=2)
+            rotated = results.tile([P, HD], F32, name="rotated")
+            nc.gpsimd.tensor_tensor(
+                out=rotated[:].rearrange("p (m a) -> p m a", a=2), in0=pairs[:, :, 0, :], in1=pairs[:, :, 1, :], op=ALU.add
+            )
             out_part = (out_0, out_1)[part]
-            nc.sync.dma_start(out=positions(out_part.flatten_outer_dims(), stream)[:, t, columns], in_=terms[0][:, columns])
+            nc.sync.dma_start(out=positions(out_part.flatten_outer_dims(), stream)[:, t, :], in_=rotated[:])
 
         v_tiles = {}
 
@@ -265,7 +267,6 @@ def tile_fluxattention_pa_kernel(
         for n in range(tiles):
             for step, part in enumerate((Q, K)):
                 s = 2 * n + step
-                fine = False
                 banks = []
                 sum_sq = stats.tile([P, HEADS], F32)
                 norm = stats.tile([P, HEADS], F32)
@@ -291,13 +292,6 @@ def tile_fluxattention_pa_kernel(
                     grouped = group(turn(n + 1))
                     operands[n + 1] = quantise(grouped)
 
-                terms = (results.tile([P, HD], F32, name="term_0"), results.tile([P, HD], F32, name="term_1"))
-                if fine:
-                    for half in range(2):
-                        products(n, part, banks, norm, terms, range(HEADS_PER_BANK * half, HEADS_PER_BANK * (half + 1)))
-                        if s == 0 and half == 0:
-                            operands[1] = quantise(grouped)
-                        add_and_store(n, part, terms, slice(BANK * half, BANK * (half + 1)))
-                else:
-                    products(n, part, banks, norm, terms, range(HEADS))
-                    add_and_store(n, part, terms, slice(0, HD))
+                terms = results.tile([P, 2 * HD], F32, name="terms")
+                products(n, part, banks, norm, terms, range(HEADS))
+                add_and_store(n, part, terms)

@@ -24,7 +24,7 @@ BANK = 512
 HEADS_PER_BANK = BANK // D
 Q, K, V = 0, 1, 2
 EPS = 1e-6
-VECTOR_TABLES = 8
+VECTOR_TABLES = 5
 
 FLOPS = 2 * 1024 * DM * 3 * HD
 
@@ -133,7 +133,8 @@ def tile_fluxattention_pa_kernel(
             nc.sync.dma_start(out=rotary[:], in_=positions(image_rotary_emb.rearrange("l i c -> l (i c)"), stream))
             stream["rotary"] = rotary
 
-        load_x(text, 0, 2)
+        load_x(text, 0, 1)
+        load_x(text, 1, 1)
         load_words(text, Q, (0, 1))
         load_scales(text)
         load_rotary(text)
@@ -151,10 +152,6 @@ def tile_fluxattention_pa_kernel(
         warm = keep.tile([P, 1], F32)
         nc.scalar.activation(out=warm[:], in_=eps[:], func=ACT.Abs_reciprocal_sqrt)
 
-        gain_bank = psum.tile([P, BANK], F32, tag="bank")
-        nc.tensor.matmul(out=gain_bank[:], lhsT=ones[:], rhs=gain_rows[:], start=True, stop=True)
-        gain_all = keep.tile([P, 4 * D], F32)
-        nc.scalar.copy(out=gain_all[:], in_=gain_bank[:])
 
         def turn(n):
             stream, t = token_tiles[n]
@@ -257,10 +254,14 @@ def tile_fluxattention_pa_kernel(
         tiles = len(token_tiles)
         operands = {}
         tables = {}
-        grouped = group(turn(0))
-        operands[0] = quantise(grouped)
+        for m in range(2):
+            operands[m] = quantise(group(turn(m)))
+        gain_bank = psum.tile([P, BANK], F32, tag="bank")
+        nc.tensor.matmul(out=gain_bank[:], lhsT=ones[:], rhs=gain_rows[:], start=True, stop=True)
+        gain_all = keep.tile([P, 4 * D], F32)
+        nc.scalar.copy(out=gain_all[:], in_=gain_bank[:])
         for m in range(VECTOR_TABLES):
-            tables[m] = make_tables(m, nc.vector, gain_all)
+            tables[m] = make_tables(m, nc.vector, gain_bank)
         for m in range(VECTOR_TABLES, tiles):
             tables[m] = make_tables(m, nc.gpsimd, gain_all)
 
@@ -288,9 +289,8 @@ def tile_fluxattention_pa_kernel(
                 if s == 2 * tiles - 1:
                     value(s)
 
-                if step == 0 and n + 1 < tiles:
-                    grouped = group(turn(n + 1))
-                    operands[n + 1] = quantise(grouped)
+                if step == 0 and 0 < n < tiles - 1:
+                    operands[n + 1] = quantise(group(turn(n + 1)))
 
                 terms = results.tile([P, 2 * HD], F32, name="terms")
                 products(n, part, banks, norm, terms, range(HEADS))

from contextlib import ExitStack

import concourse.mybir as mybir
from concourse.masks import make_identity

F32 = mybir.dt.float32
BF16 = mybir.dt.bfloat16
I32 = mybir.dt.int32
U32 = mybir.dt.uint32
U8 = mybir.dt.uint8
FP8X4 = mybir.dt.float8_e4m3fn_x4
FP4X4 = mybir.dt.float4_e2m1fn_x4
ACT = mybir.ActivationFunctionType
ALU = mybir.AluOpType

P = 128
PACK = 4
DM = 1024
PASSES = DM // (P * PACK)
HEADS = 8
D = 128
HD = HEADS * D
BANK = 512
HEADS_PER_BANK = BANK // D
Q, K, V = 0, 1, 2
EPS = 1e-6
VECTOR_TABLES = 5

FLOPS = 2 * 1024 * DM * 3 * HD


def tile_fluxattention_pa_kernel(
    tc,
    hidden_states,
    encoder_hidden_states,
    image_rotary_emb,
    W_iqkv_words,
    W_iqkv_scales,
    W_eqkv_words,
    W_eqkv_scales,
    qn_scale,
    kn_scale,
    eqn_scale,
    ekn_scale,
    out_0,
    out_1,
    out_2,
):
    nc = tc.nc

    text = {
        "name": "text",
        "x": encoder_hidden_states.flatten_outer_dims(),
        "words": W_eqkv_words,
        "scales": W_eqkv_scales,
        "first": 0,
        "tiles": 2,
        "gain_slot": 0,
    }
    image = {
        "name": "image",
        "x": hidden_states.flatten_outer_dims(),
        "words": W_iqkv_words,
        "scales": W_iqkv_scales,
        "first": 256,
        "tiles": 6,
        "gain_slot": 2,
    }
    gains = (eqn_scale, ekn_scale, qn_scale, kn_scale)
    token_tiles = [(stream, t) for stream in (text, image) for t in range(stream["tiles"])]

    def by_tile(rows, stream):
        return rows.rearrange("(p t) w -> p t w", t=stream["tiles"])

    def positions(rows, stream):
        return by_tile(rows[stream["first"] : stream["first"] + P * stream["tiles"], :], stream)

    with ExitStack() as ctx:
        keep = ctx.enter_context(tc.tile_pool(name="keep", bufs=1))
        stage = ctx.enter_context(tc.tile_pool(name="stage", bufs=2))
        quantised = ctx.enter_context(tc.tile_pool(name="quantised", bufs=3))
        stats = ctx.enter_context(tc.tile_pool(name="stats", bufs=4))
        squares = ctx.enter_context(tc.tile_pool(name="squares", bufs=2))
        results = ctx.enter_context(tc.tile_pool(name="results", bufs=4))
        psum = ctx.enter_context(tc.psum_pool(name="psum", bufs=8))
        ctx.enter_context(tc.manual_schedule())

        gain_rows = keep.tile([P, 4 * D], BF16)
        nc.vector.memset(gain_rows[:], 0.0)
        for slot, gain in enumerate(gains):
            nc.scalar.dma_start(out=gain_rows[0:1, slot * D : (slot + 1) * D], in_=gain.unsqueeze(0))
        ones = keep.tile([P, P], BF16)
        nc.vector.memset(ones[:], 1.0)
        eps = keep.tile([P, 1], F32)
        nc.vector.memset(eps[:], EPS)

        identity = keep.tile([P, P], F32)
        make_identity(nc, identity[:])

        for stream in (text, image):
            stream["planes"] = keep.tile([P, PASSES, 3 * HD], U8, name="planes_%s" % stream["name"], align_bytes=64)
            nc.vector.memset(stream["planes"][:].bitcast(I32), 0)
            stream["x_sb"] = {}
            stream["words_sb"] = {}

        def load_x(stream, first, count):
            x_sb = keep.tile([P, count, DM], BF16, name="x_%s_%d" % (stream["name"], first))
            nc.sync.dma_start(out=x_sb[:], in_=by_tile(stream["x"], stream)[:, first : first + count, :])
            for j in range(count):
                stream["x_sb"][first + j] = x_sb[:, j, :]

        def load_words(stream, part, halves):
            width = len(halves) * BANK
            words = keep.tile(
                [P, PASSES, 2 * width], U8, name="words_%s_%d_%d" % (stream["name"], part, halves[0]), align_bytes=64
            )
            start = (part * HD + halves[0] * BANK) // 2
            source = stream["words"].bitcast(I32)[:, :, start : start + width // 2]
            nc.sync.dma_start(out=words[:].bitcast(I32), in_=source.rearrange("g p w -> p g w"))
            for j, half in enumerate(halves):
                stream["words_sb"][(part, half)] = words[:, :, 2 * BANK * j : 2 * BANK * (j + 1)]

        def load_scales(stream):
            source = stream["scales"].bitcast(I32)
            for quadrant in range(4):
                nc.sync.dma_start(
                    out=stream["planes"][32 * quadrant : 32 * quadrant + 4, :, :].bitcast(I32),
                    in_=source[:, 4 * quadrant : 4 * quadrant + 4, :].rearrange("g r n -> r g n"),
                )

        def load_rotary(stream):
            rotary = keep.tile([P, stream["tiles"], 2 * D], BF16, name="rotary_%s" % stream["name"])
            nc.sync.dma_start(out=rotary[:], in_=positions(image_rotary_emb.rearrange("l i c -> l (i c)"), stream))
            stream["rotary"] = rotary

        load_x(text, 0, 1)
        load_x(text, 1, 1)
        load_words(text, Q, (0, 1))
        load_scales(text)
        load_rotary(text)
        load_rotary(image)
        load_words(text, V, (0, 1))
        load_words(text, K, (0, 1))
        load_x(image, 0, 2)
        load_scales(image)
        load_words(image, Q, (0, 1))
        load_words(image, V, (0, 1))
        load_words(image, K, (0, 1))
        load_x(image, 2, 2)
        load_x(image, 4, 2)

        warm = keep.tile([P, 1], F32)
        nc.scalar.activation(out=warm[:], in_=eps[:], func=ACT.Abs_reciprocal_sqrt)


        def turn(n):
            stream, t = token_tiles[n]
            x_words = stream["x_sb"][t].bitcast(F32)
            turned = psum.tile([P, BANK], F32, tag="bank")
            for g in range(PASSES):
                for u in range(2):
                    nc.tensor.transpose(
                        turned[:, (2 * g + u) * P : (2 * g + u + 1) * P],
                        x_words[:, 256 * g + u : 256 * (g + 1) : 2],
                        identity[:],
                    )
            return turned

        def group(turned):
            grouped = stage.tile([P, PASSES * P * PACK], BF16, align_bytes=64)
            nc.scalar.copy(
                out=grouped[:].bitcast(F32).rearrange("p (g r u) -> p g r u", g=PASSES, u=2),
                in_=turned[:].rearrange("p (g u r) -> p g r u", g=PASSES, u=2),
            )
            return grouped

        def quantise(grouped):
            x_codes = quantised.tile([P, PASSES * P], U32, align_bytes=64)
            x_scales = quantised.tile([P, PASSES * P], U8, align_bytes=64)
            nc.vector.quantize_mx(out=x_codes[:].bitcast(FP8X4), scales=x_scales[:], in_=grouped[:])
            return x_codes, x_scales

        def make_tables(n, engine, gain_source):
            stream, t = token_tiles[n]
            table = keep.tile([P, 2, 2 * D], F32, name="table_%d" % n)
            matrices = stream["rotary"][:, t, :].rearrange("p (i a b) -> p i b a", a=2, b=2)
            for part in (Q, K):
                slot = stream["gain_slot"] + part
                gain = gain_source[:, slot * D : (slot + 1) * D].rearrange("p (i b) -> p i b", b=2)
                engine.tensor_tensor(
                    out=table[:, part, :].rearrange("p (i b a) -> p i b a", a=2, b=2),
                    in0=matrices,
                    in1=gain.unsqueeze(3).to_broadcast([P, D // 2, 2, 2]),
                    op=ALU.mult,
                )
            return table

        def project(n, operands, part, half):
            stream = token_tiles[n][0]
            x_codes, x_scales = operands
            acc = psum.tile([P, BANK], F32, tag="bank")
            for g in range(PASSES):
                nc.tensor.matmul_mx(
                    out=acc[:],
                    lhsT=x_codes[:, g * P : (g + 1) * P].bitcast(FP8X4),
                    lhsT_scale=x_scales[:, g * P : (g + 1) * P],
                    rhs=stream["words_sb"][(part, half)][:, g, :].bitcast(FP4X4),
                    rhs_scale=stream["planes"][:, g, part * HD + BANK * half : part * HD + BANK * (half + 1)],
                    start=(g == 0),
                    stop=(g == PASSES - 1),
                )
            return acc

        def root(norm, sum_sq, heads):
            nc.scalar.activation(
                out=norm[:, heads], in_=sum_sq[:, heads], func=ACT.Abs_reciprocal_sqrt, bias=eps[:], scale=1.0 / D
            )

        def products(n, part, banks, norm, terms, heads):
            for h in heads:
                j = h % HEADS_PER_BANK
                nc.vector.scalar_tensor_tensor(
                    out=terms[:, 2 * h * D : 2 * (h + 1) * D].rearrange("p (f a) -> p f a", a=2),
                    in0=banks[h // HEADS_PER_BANK][:, j * D : (j + 1) * D].unsqueeze(2).to_broadcast([P, D, 2]),
                    scalar=norm[:, h : h + 1],
                    in1=tables[n][:, part, :].rearrange("p (f a) -> p f a", a=2),
                    op0=ALU.mult,
                    op1=ALU.mult,
                )

        def add_and_store(n, part, terms):
            stream, t = token_tiles[n]
            pairs = terms[:].rearrange("p (m b a) -> p m b a", a=2, b=2)
            rotated = results.tile([P, HD], F32, name="rotated")
            nc.gpsimd.tensor_tensor(
                out=rotated[:].rearrange("p (m a) -> p m a", a=2), in0=pairs[:, :, 0, :], in1=pairs[:, :, 1, :], op=ALU.add
            )
            out_part = (out_0, out_1)[part]
            nc.sync.dma_start(out=positions(out_part.flatten_outer_dims(), stream)[:, t, :], in_=rotated[:])

        v_tiles = {}

        def value(unit):
            n, half = unit // 2, unit % 2
            stream, t = token_tiles[n]
            if half == 0:
                v_sb = results.tile([P, HD], F32, name="v_sb")
                v_tiles[n] = v_sb
            v_acc = project(n, operands[n], V, half)
            nc.scalar.copy(out=v_tiles[n][:, half * BANK : (half + 1) * BANK], in_=v_acc[:])
            if half == 1:
                nc.sync.dma_start(out=positions(out_2.flatten_outer_dims(), stream)[:, t, :], in_=v_tiles[n][:])

        tiles = len(token_tiles)
        operands = {}
        tables = {}
        for m in range(2):
            operands[m] = quantise(group(turn(m)))
        gain_bank = psum.tile([P, BANK], F32, tag="bank")
        nc.tensor.matmul(out=gain_bank[:], lhsT=ones[:], rhs=gain_rows[:], start=True, stop=True)
        gain_all = keep.tile([P, 4 * D], F32)
        nc.scalar.copy(out=gain_all[:], in_=gain_bank[:])
        for m in range(VECTOR_TABLES):
            tables[m] = make_tables(m, nc.vector, gain_bank)
        for m in range(VECTOR_TABLES, tiles):
            tables[m] = make_tables(m, nc.gpsimd, gain_all)

        for n in range(tiles):
            for step, part in enumerate((Q, K)):
                s = 2 * n + step
                banks = []
                sum_sq = stats.tile([P, HEADS], F32)
                norm = stats.tile([P, HEADS], F32)
                unused = squares.tile([P, HEADS, D], BF16)
                for half in range(2):
                    acc = project(n, operands[n], part, half)
                    banks.append(acc)
                    for j in range(HEADS_PER_BANK):
                        h = HEADS_PER_BANK * half + j
                        nc.scalar.activation(
                            out=unused[:, h, :],
                            in_=acc[:, j * D : (j + 1) * D],
                            func=ACT.Square,
                            accum_out=sum_sq[:, h : h + 1],
                        )
                if s >= 1:
                    value(s - 1)
                root(norm, sum_sq, slice(0, HEADS))
                if s == 2 * tiles - 1:
                    value(s)

                if step == 0 and 0 < n < tiles - 1:
                    operands[n + 1] = quantise(group(turn(n + 1)))

                terms = results.tile([P, 2 * HD], F32, name="terms")
                products(n, part, banks, norm, terms, range(HEADS))
                add_and_store(n, part, terms)
